import numpy as np
import ml_dtypes


def mxq(x, axis, fmt="e4m3"):
    dtype, down = {"e4m3": (ml_dtypes.float8_e4m3fn, 7), "e5m2": (ml_dtypes.float8_e5m2, 14)}[fmt]
    v = np.moveaxis(np.asarray(x, np.float32).astype(ml_dtypes.bfloat16).astype(np.float64), axis, -1)
    blocks = v.reshape(v.shape[:-1] + (-1, 32))
    amax = np.abs(blocks).max(-1, keepdims=True)
    byte = np.maximum(np.where(amax > 0, np.frexp(amax)[1] - 1 + 127, 0) - down, 1)
    scale = np.exp2(byte - 127.0)
    codes = (blocks / scale).astype(np.float32).astype(dtype).astype(np.float64)
    return np.moveaxis((codes * scale).reshape(v.shape), -1, axis)


WIDE = False


def mx_kscale(k):
    if not WIDE:
        return np.ones(k)
    levels = np.array([10, -10, 5, -5, 0])
    if k % 512:
        return np.exp2(np.random.permutation(np.resize(levels, k // 32))).repeat(32)
    a = np.empty((k // 512, 16))
    for p in range(k // 512):
        a[p, :8] = np.random.permutation(np.resize(levels, 8))
        for g in range(8):
            far = levels[np.abs(levels - a[p, g]) >= 10]
            a[p, g + 8] = far[np.random.randint(len(far))]
    return np.exp2(a.ravel()).repeat(32)


BF16 = ml_dtypes.bfloat16


def bf(x):
    return np.asarray(x, np.float32).astype(BF16)


def f64(x):
    return np.asarray(x).astype(np.float64)


E2M1 = np.array([0.0, 0.5, 1.0, 1.5, 2.0, 3.0, 4.0, 6.0, -0.0, -0.5, -1.0, -1.5, -2.0, -3.0, -4.0, -6.0])


def pack_weight(w, fmt):
    k, n = w.shape
    w = f64(bf(w)).reshape(k // 32, 32, n)
    amax = np.abs(w).max(1)
    if fmt == "e4m3":
        byte = np.frexp(amax)[1] - 1 + 127 - 7
    else:
        mant, ex = np.frexp(amax / 6.0)
        byte = np.where(mant > 0.5, ex, ex - 1) + 127
    byte = np.clip(np.where(amax > 0, byte, 1), 1, 254)
    scaled = (w * np.exp2(127.0 - byte)[:, None, :]).reshape(k, n).astype(np.float32)
    by_word = np.ascontiguousarray(scaled.reshape(k // 512, 128, 4, n).transpose(0, 1, 3, 2))
    if fmt == "e4m3":
        words = by_word.astype(ml_dtypes.float8_e4m3fn).view(np.uint8)
    else:
        c = by_word.astype(ml_dtypes.float4_e2m1fn).view(np.uint8) & 0xF
        words = c[..., 0::2] | (c[..., 1::2] << 4)
    return np.ascontiguousarray(words), np.ascontiguousarray(byte.astype(np.uint8).reshape(k // 512, 16, n))


def unpack_weight(words, scales, fmt):
    g, p, n, _ = words.shape
    if fmt == "e4m3":
        vals = np.ascontiguousarray(words).view(ml_dtypes.float8_e4m3fn).astype(np.float64)
    else:
        nib = np.empty((g, p, n, 4), np.uint8)
        nib[..., 0::2] = words & 0xF
        nib[..., 1::2] = words >> 4
        vals = E2M1[nib]
    vals = vals * np.repeat(np.exp2(scales.astype(np.float64) - 127.0), 8, axis=1)[..., None]
    return vals.transpose(0, 1, 3, 2).reshape(g * 512, n)
def pack4(w):
    words, scales = pack_weight(w, "e2m1")
    return words.reshape(words.shape[0], 128, -1), scales


def unpack4(words, scales):
    return unpack_weight(words.reshape(words.shape[0], 128, -1, 2), scales, "e2m1")


B, S, D, E, F = 4, 1024, 512, 1024, 256
EPS = 1e-5


def layernorm(x, g, b):
    m = x.mean(-1, keepdims=True)
    v = ((x - m) ** 2).mean(-1, keepdims=True)
    return (x - m) * (1.0 / np.sqrt(v + EPS)) * g + b


def draw0():
    s, t = mx_kscale(E), mx_kscale(D)
    attn = bf(0.4 * np.random.standard_normal((B, S, E)) * s)
    src_norm = bf(np.random.standard_normal((B, S, D)) + 0.3)
    Wo_words, Wo_scales = pack4((np.random.standard_normal((D, E)) / np.sqrt(E) / s[None, :]).T)
    bo = bf(0.1 * np.random.standard_normal(D))
    g2 = bf((1.0 + 0.1 * np.random.standard_normal(D)) * t)
    be2 = bf(0.1 * np.random.standard_normal(D) * t)
    W1_words, W1_scales = pack4((np.random.standard_normal((F, D)) / np.sqrt(D) / t[None, :]).T)
    b1 = bf(0.1 * np.random.standard_normal(F))
    return {"attn": attn,
            "src_norm": src_norm,
            "Wo_words": Wo_words,
            "Wo_scales": Wo_scales,
            "bo": bo,
            "g2": g2,
            "be2": be2,
            "W1_words": W1_words,
            "W1_scales": W1_scales,
            "b1": b1}


def core(attn, src_norm, Wo_words, Wo_scales, bo, g2, be2, W1_words, W1_scales, b1):
    x = f64(src_norm) + (mxq(f64(attn), 2, "e4m3") @ unpack4(Wo_words, Wo_scales)) + f64(bo)
    h = layernorm(x, f64(g2), f64(be2))
    u = np.maximum((mxq(h, 2, "e4m3") @ unpack4(W1_words, W1_scales)) + f64(b1), 0.0)
    return x, u


def e4m3fn_bytes(y):
    return np.clip(np.asarray(y, np.float64), -448.0, 448.0).astype(np.float32).astype(ml_dtypes.float8_e4m3fn).view(np.uint8)


def e4m3fn_values(b):
    return np.asarray(b, np.uint8).view(ml_dtypes.float8_e4m3fn).astype(np.float64)


def setup_inputs():
    d = draw0()
    x0 = np.asarray(d['attn']).astype(np.float64)
    s = (np.max(np.abs(x0), axis=(0, 1), keepdims=True) / 448.0).astype(np.float32)
    out = {}
    for k, v in d.items():
        if k == 'attn':
            out['attn_bytes'] = e4m3fn_bytes(x0 / s.astype(np.float64))
            out['attn_scale'] = s
        else:
            out[k] = v
    return out


def reference(attn_bytes, attn_scale, src_norm, Wo_words, Wo_scales, bo, g2, be2, W1_words, W1_scales, b1):
    return core(e4m3fn_values(attn_bytes) * attn_scale.astype(np.float64), src_norm, Wo_words, Wo_scales, bo, g2, be2, W1_words, W1_scales, b1)

@@ -1,0 +1,320 @@
+from contextlib import ExitStack
+
+import concourse.mybir as mybir
+from concourse.masks import make_identity
+
+F32 = mybir.dt.float32
+BF16 = mybir.dt.bfloat16
+U8 = mybir.dt.uint8
+U32 = mybir.dt.uint32
+I32 = mybir.dt.int32
+FP8 = mybir.dt.float8_e4m3fn
+FP8X4 = mybir.dt.float8_e4m3fn_x4
+FP4X4 = mybir.dt.float4_e2m1fn_x4
+ADD = mybir.AluOpType.add
+SUB = mybir.AluOpType.subtract
+MULT = mybir.AluOpType.mult
+MAX = mybir.AluOpType.max
+POW = mybir.AluOpType.pow
+COPY = mybir.ActivationFunctionType.Copy
+IDENT = mybir.ActivationFunctionType.Identity
+SQUARE = mybir.ActivationFunctionType.Square
+RELU = mybir.ActivationFunctionType.Relu
+RELU_ON_SCALAR = []
+
+P = 128
+TOKENS, D, E, F = 4096, 512, 1024, 256
+PAIRS = TOKENS // 256
+EPS = 1e-5
+FLOPS = 2 * TOKENS * (E * D + D * F)
+
+SLOT = (
+    ("IL", 1, 6),
+    ("M2", 0, 8),
+    ("SQ", 0, 4),
+    ("SQ", 1, 4),
+    ("QA", 0, 2),
+    ("XA", 1, 3),
+    ("TH", 0, 5),
+    ("TH", 1, 5),
+    ("IL", 0, 6),
+    ("EH", 2, 5),
+    ("XA", 0, 3),
+    ("EH", 0, 5),
+    ("P", 0, 0),
+    ("RL", 0, 10),
+    ("TA", 1, 1),
+    ("EA", 1, 1),
+    ("EH", 1, 5),
+    ("UA", 0, 8),
+    ("QB", 0, 7),
+    ("TA", 0, 1),
+    ("XH", 0, 4),
+    ("MM", 1, 2),
+    ("XH", 1, 4),
+    ("MM", 0, 2),
+    ("P", 1, 0),
+    ("SB", 0, 2),
+    ("EH", 3, 5),
+    ("EA", 0, 1),
+)
+X_HAT_ON_VECTOR = [26,27,28,29,30,31]
+
+
+def tile_rotaryembeddingtransformerlayer_pb_t_w4_kernel(
+    tc, attn_bytes, attn_scale, src_norm, Wo_words, Wo_scales, bo, g2, be2, W1_words, W1_scales, b1, x_out, u_out
+):
+    nc = tc.nc
+    bytes_in = attn_bytes.flatten_outer_dims().rearrange("(q p r) k -> q p (r k)", p=P, r=4)
+    src_in = src_norm.flatten_outer_dims().rearrange("(q p r) d -> q p (r d)", p=P, r=4)
+    x_hbm = x_out.flatten_outer_dims().rearrange("(q p r) d -> q p (r d)", p=P, r=4)
+    u_hbm = u_out.flatten_outer_dims().rearrange("(q p r) f -> q p (r f)", p=P, r=4)
+
+    with ExitStack() as ctx:
+        const = ctx.enter_context(tc.tile_pool(name="const", bufs=1))
+        work = ctx.enter_context(tc.tile_pool(name="work", bufs=2))
+        psum = ctx.enter_context(tc.psum_pool(name="psum", bufs=1))
+        ctx.enter_context(tc.manual_schedule())
+
+        warm = const.tile([P, 1], F32)
+        nc.vector.memset(warm[:], 0.0)
+        scale = const.tile([P, E], F32)
+        nc.scalar.dma_start(out=scale[:], in_=attn_scale.rearrange("a b k -> (a b k)").partition_broadcast(P))
+        byte_tiles = [const.tile([P, 2 * E], U8, name="bytes%d" % n) for n in range(PAIRS)]
+        src_tiles = [const.tile([P, 4 * D], BF16, name="src%d" % n) for n in range(PAIRS // 2)]
+        wo = const.tile([P, 2, 2 * D], U8, align_bytes=64)
+        wo_s = const.tile([P, 2, D], U8, align_bytes=64)
+        w1 = const.tile([P, 2 * F], U8, align_bytes=64)
+        w1_s = const.tile([P, F], U8, align_bytes=64)
+        bo_row = const.tile([P, D], BF16)
+        b1_row = const.tile([P, F], BF16)
+        g2_raw = const.tile([P, 4], BF16)
+        be2_raw = const.tile([P, 4], BF16)
+        g2_col = const.tile([P, 4], F32)
+        be2_col = const.tile([P, 4], F32)
+        half = const.tile([P, 2], F32)
+        identity = const.tile([P, P], F32)
+
+        def load_bytes(n):
+            nc.sync.dma_start(out=byte_tiles[n][:], in_=bytes_in[n // 2][:, (n % 2) * 2 * E : (n % 2 + 1) * 2 * E])
+
+        nc.vector.memset(wo_s[:].rearrange("p g n -> p (g n)").bitcast(I32), 0)
+        nc.vector.memset(w1_s[:].bitcast(I32), 0)
+        nc.gpsimd.memset(half[:], -0.5)
+        load_bytes(0)
+        nc.scalar.activation(out=warm[:], in_=warm[:], func=SQUARE)
+        make_identity(nc, identity[:])
+        load_bytes(1)
+        nc.sync.dma_start(out=wo[:], in_=Wo_words.rearrange("g p b -> p g b"))
+        for Q in range(4):
+            nc.sync.dma_start(
+                out=wo_s[32 * Q : 32 * Q + 4].bitcast(I32),
+                in_=Wo_scales[:, 4 * Q : 4 * Q + 4, :].rearrange("g q n -> q g n").bitcast(I32),
+            )
+        nc.scalar.dma_start(out=bo_row[:], in_=bo.partition_broadcast(P))
+        nc.sync.dma_start(out=src_tiles[0][:], in_=src_in[0])
+        nc.scalar.dma_start(out=g2_raw[:], in_=g2.rearrange("(p t) -> p t", t=4))
+        nc.scalar.dma_start(out=be2_raw[:], in_=be2.rearrange("(p t) -> p t", t=4))
+        nc.scalar.dma_start(out=b1_row[:], in_=b1.partition_broadcast(P))
+        load_bytes(2)
+        load_bytes(3)
+        nc.sync.dma_start(out=w1[:], in_=W1_words[0])
+        for Q in range(4):
+            nc.sync.dma_start(
+                out=w1_s[32 * Q : 32 * Q + 4].bitcast(I32), in_=W1_scales[0, 4 * Q : 4 * Q + 4, :].bitcast(I32)
+            )
+        for n in range(4, PAIRS, 2):
+            nc.sync.dma_start(out=src_tiles[n // 2 - 1][:], in_=src_in[n // 2 - 1])
+            load_bytes(n)
+            load_bytes(n + 1)
+        nc.sync.dma_start(out=src_tiles[PAIRS // 2 - 1][:], in_=src_in[PAIRS // 2 - 1])
+        nc.gpsimd.tensor_copy(out=g2_col[:], in_=g2_raw[:])
+        nc.gpsimd.tensor_copy(out=be2_col[:], in_=be2_raw[:])
+
+        t = {}
+
+        def product(n, i):
+            a = work.tile([P, E], BF16, name="a", tag="a", bufs=4)
+            t["a", n, i] = a
+            nc.vector.tensor_tensor(
+                out=a[:], in0=byte_tiles[n][:, i * E : (i + 1) * E].bitcast(FP8), in1=scale[:], op=MULT
+            )
+
+        def turn_a(n, i):
+            at = psum.tile([P, 2, 2, P], F32, name="at", tag="at", bufs=2)
+            t["at", n, i] = at
+            words = t["a", n, i][:].bitcast(F32)
+            for g in range(2):
+                for j in range(2):
+                    nc.tensor.transpose(at[:, g, j, :], words[:, 256 * g + j : 256 * (g + 1) : 2], identity[:])
+
+        def empty_a(n, i):
+            if ("ag", n) not in t:
+                t["ag", n] = work.tile([P, 2, 512], F32, name="ag", tag="ag", bufs=3, align_bytes=64)
+            nc.scalar.copy(
+                out=t["ag", n][:, i, :].rearrange("p (g r u) -> p g r u", g=2, u=2),
+                in_=t["at", n, i][:].rearrange("p g u r -> p g r u"),
+            )
+
+        def quantise_a(n, i):
+            t["ac", n] = work.tile([P, 512], U32, name="ac", tag="ac", bufs=3, align_bytes=64)
+            t["as", n] = work.tile([P, 512], U8, name="as_", tag="as", bufs=3, align_bytes=64)
+            nc.vector.quantize_mx(
+                out=t["ac", n][:].bitcast(FP8X4),
+                scales=t["as", n][:],
+                in_=t["ag", n][:].rearrange("p i w -> p (i w)").bitcast(BF16),
+            )
+
+        def multiply_a(n, i):
+            y = psum.tile([P, D], F32, name="y", tag="y", bufs=3)
+            t["y", n, i] = y
+            for g in range(2):
+                cols = slice((2 * i + g) * P, (2 * i + g + 1) * P)
+                nc.tensor.matmul_mx(
+                    out=y[:],
+                    lhsT=t["ac", n][:, cols].bitcast(FP8X4),
+                    lhsT_scale=t["as", n][:, cols],
+                    rhs=wo[:, g, :].bitcast(FP4X4),
+                    rhs_scale=wo_s[:, g, :],
+                    start=(g == 0),
+                    stop=(g == 1),
+                )
+
+        def add_bias(n, i):
+            sb = work.tile([P, 2, D], F32, name="sb", tag="sb", bufs=3)
+            t["sb", n] = sb
+            nc.vector.tensor_tensor(
+                out=sb[:],
+                in0=src_tiles[n // 2][:, (n % 2) * 2 * D : (n % 2 + 1) * 2 * D].rearrange("p (r d) -> p r d", r=2),
+                in1=bo_row[:].unsqueeze(1).to_broadcast([P, 2, D]),
+                op=ADD,
+            )
+
+        def add_x(n, i):
+            if ("x", n) not in t:
+                t["x", n] = work.tile([P, 2, D], F32, name="x", tag="x", bufs=5)
+                t["sum", n] = work.tile([P, 2], F32, name="sum_", tag="sum", bufs=4)
+                t["nm", n] = work.tile([P, 2], F32, name="nm", tag="nm", bufs=4)
+                t["sq", n] = work.tile([P, 2], F32, name="sq", tag="sq", bufs=4)
+                t["st", n] = work.tile([P, 3, 2], F32, name="st", tag="st", bufs=4)
+            nc.vector.scalar_tensor_tensor(
+                out=t["x", n][:, i, :],
+                in0=t["y", n, i][:],
+                scalar=1.0,
+                in1=t["sb", n][:, i, :],
+                op0=MULT,
+                op1=ADD,
+                accum_out=t["sum", n][:, i : i + 1],
+            )
+            if ("xdone", n) in t:
+                nc.gpsimd.tensor_scalar(
+                    out=t["nm", n][:], in0=t["sum", n][:], scalar1=-1.0 / D, scalar2=0.0, op0=MULT, op1=ADD
+                )
+                nc.sync.dma_start(
+                    out=x_hbm[n // 2][:, (n % 2) * 2 * D : (n % 2 + 1) * 2 * D],
+                    in_=t["x", n][:].rearrange("p r d -> p (r d)"),
+                )
+            t["xdone", n] = True
+
+        def square(n, i):
+            junk = work.tile([P, D], BF16, name="junk", tag="junk", bufs=2)
+            nc.scalar.activation(
+                out=junk[:],
+                in_=t["x", n][:, i, :],
+                func=SQUARE,
+                bias=t["nm", n][:, i : i + 1],
+                accum_out=t["sq", n][:, i : i + 1],
+            )
+            if ("sqdone", n) in t:
+                st = t["st", n]
+                nc.gpsimd.tensor_scalar(
+                    out=st[:, 0, :], in0=t["sq", n][:], scalar1=1.0 / D, scalar2=EPS, op0=MULT, op1=ADD
+                )
+                nc.gpsimd.tensor_tensor(out=st[:, 1, :], in0=st[:, 0, :], in1=half[:], op=POW)
+                nc.gpsimd.tensor_tensor(out=st[:, 2, :], in0=t["nm", n][:], in1=st[:, 1, :], op=MULT)
+            t["sqdone", n] = True
+
+        def normalise(n, i):
+            xh = work.tile([P, 4, P], F32, name="xh", tag="xh", bufs=4)
+            t["xh", n, i] = xh
+            x = t["x", n][:, i, :].rearrange("p (m t) -> p t m", t=4)
+            st = t["st", n]
+            if 2 * n + i in X_HAT_ON_VECTOR:
+                nc.vector.tensor_scalar(
+                    out=xh[:], in0=x, scalar1=t["nm", n][:, i : i + 1], scalar2=st[:, 1, i : i + 1], op0=ADD, op1=MULT
+                )
+            else:
+                nc.scalar.activation(out=xh[:], in_=x, func=IDENT, scale=st[:, 1, i : i + 1], bias=st[:, 2, i : i + 1])
+
+        def turn_h(n, i):
+            if ("ht", n, 0) not in t:
+                for b in range(2):
+                    t["ht", n, b] = psum.tile([P, 2, 2, P], F32, name="ht", tag="ht", bufs=2)
+            for c in range(4):
+                nc.tensor.transpose(t["ht", n, c // 2][:, c % 2, i, :], t["xh", n, i][:, c, :], identity[:])
+
+        def empty_h(n, c):
+            if ("hp", n) not in t:
+                t["hp", n] = work.tile([P, 4, 256], BF16, name="hp", tag="hp", bufs=4)
+            nc.scalar.activation(
+                out=t["hp", n][:, c, :],
+                in_=t["ht", n, c // 2][:, c % 2, :, :].rearrange("p i r -> p (i r)"),
+                func=IDENT,
+                scale=g2_col[:, c : c + 1],
+                bias=be2_col[:, c : c + 1],
+            )
+
+        def interleave(n, i):
+            if ("hg", n) not in t:
+                t["hg", n] = work.tile([P, 1024], BF16, name="hg", tag="hg", bufs=3, align_bytes=64)
+            nc.scalar.copy(
+                out=t["hg", n][:, i * 512 : (i + 1) * 512].rearrange("p (c s t) -> p c t s", s=4, t=4),
+                in_=t["hp", n][:, :, i * P : (i + 1) * P].rearrange("p t (c s) -> p c t s", s=4),
+            )
+
+        def quantise_h(n, i):
+            t["hc", n] = work.tile([P, 256], U32, name="hc", tag="hc", bufs=3, align_bytes=64)
+            t["hs", n] = work.tile([P, 256], U8, name="hs", tag="hs", bufs=3, align_bytes=64)
+            nc.vector.quantize_mx(out=t["hc", n][:].bitcast(FP8X4), scales=t["hs", n][:], in_=t["hg", n][:])
+
+        def multiply_h(n, i):
+            up = psum.tile([P, 2, F], F32, name="up", tag="up", bufs=1)
+            t["up", n] = up
+            for r in range(2):
+                cols = slice(r * P, (r + 1) * P)
+                nc.tensor.matmul_mx(
+                    out=up[:, r, :],
+                    lhsT=t["hc", n][:, cols].bitcast(FP8X4),
+                    lhsT_scale=t["hs", n][:, cols],
+                    rhs=w1[:].bitcast(FP4X4),
+                    rhs_scale=w1_s[:],
+                    start=True,
+                    stop=True,
+                )
+
+        def add_u(n, i):
+            us = work.tile([P, 2, F], F32, name="us", tag="us", bufs=4)
+            t["us", n] = us
+            nc.vector.tensor_tensor(
+                out=us[:], in0=t["up", n][:], in1=b1_row[:].unsqueeze(1).to_broadcast([P, 2, F]), op=ADD
+            )
+
+        def relu_u(n, i):
+            uo = work.tile([P, 2, F], F32, name="uo", tag="uo", bufs=3)
+            if n in RELU_ON_SCALAR:
+                nc.scalar.activation(out=uo[:], in_=t["us", n][:], func=RELU)
+            else:
+                nc.vector.tensor_scalar(out=uo[:], in0=t["us", n][:], scalar1=0.0, scalar2=None, op0=MAX)
+            nc.sync.dma_start(
+                out=u_hbm[n // 2][:, (n % 2) * 2 * F : (n % 2 + 1) * 2 * F], in_=uo[:].rearrange("p r f -> p (r f)")
+            )
+
+        stages = {
+            "P": product, "TA": turn_a, "EA": empty_a, "QA": quantise_a, "MM": multiply_a, "SB": add_bias,
+            "XA": add_x, "SQ": square, "XH": normalise, "TH": turn_h, "EH": empty_h, "IL": interleave,
+            "QB": quantise_h, "M2": multiply_h, "UA": add_u, "RL": relu_u,
+        }
+        for s in range(PAIRS + max(lag for a, b, lag in SLOT)):
+            for name, i, lag in SLOT:
+                if 0 <= s - lag < PAIRS:
+                    stages[name](s - lag, i)

@@ -12,15 +12,12 @@ FP8 = mybir.dt.float8_e4m3fn
 FP8X4 = mybir.dt.float8_e4m3fn_x4
 FP4X4 = mybir.dt.float4_e2m1fn_x4
 ADD = mybir.AluOpType.add
-SUB = mybir.AluOpType.subtract
 MULT = mybir.AluOpType.mult
 MAX = mybir.AluOpType.max
-POW = mybir.AluOpType.pow
-COPY = mybir.ActivationFunctionType.Copy
 IDENT = mybir.ActivationFunctionType.Identity
 SQUARE = mybir.ActivationFunctionType.Square
 RELU = mybir.ActivationFunctionType.Relu
-RELU_ON_SCALAR = []
+ARS = mybir.ActivationFunctionType.Abs_reciprocal_sqrt
 
 P = 128
 TOKENS, D, E, F = 4096, 512, 1024, 256
@@ -29,36 +26,40 @@ EPS = 1e-5
 FLOPS = 2 * TOKENS * (E * D + D * F)
 
 SLOT = (
-    ("IL", 1, 6),
-    ("M2", 0, 8),
-    ("SQ", 0, 4),
-    ("SQ", 1, 4),
-    ("QA", 0, 2),
-    ("XA", 1, 3),
-    ("TH", 0, 5),
-    ("TH", 1, 5),
-    ("IL", 0, 6),
-    ("EH", 2, 5),
-    ("XA", 0, 3),
-    ("EH", 0, 5),
-    ("P", 0, 0),
-    ("RL", 0, 10),
+    ("XA", 1, 4),
+    ("SQ", 0, 5),
     ("TA", 1, 1),
-    ("EA", 1, 1),
-    ("EH", 1, 5),
-    ("UA", 0, 8),
-    ("QB", 0, 7),
-    ("TA", 0, 1),
-    ("XH", 0, 4),
-    ("MM", 1, 2),
-    ("XH", 1, 4),
-    ("MM", 0, 2),
+    ("XA", 0, 4),
+    ("MM", 1, 3),
+    ("MM", 0, 3),
+    ("EH", 2, 7),
+    ("AR", 0, 5),
+    ("EH", 3, 7),
+    ("M2", 0, 13),
+    ("XH", 1, 6),
+    ("QB", 0, 11),
+    ("NM", 0, 5),
+    ("P", 0, 0),
+    ("IL", 0, 9),
+    ("EH", 1, 7),
+    ("EH", 0, 7),
+    ("NR", 0, 5),
+    ("TH", 1, 6),
+    ("SB", 0, 3),
+    ("RL", 0, 16),
+    ("TH", 0, 6),
+    ("QA", 0, 2),
     ("P", 1, 0),
-    ("SB", 0, 2),
-    ("EH", 3, 5),
     ("EA", 0, 1),
+    ("UA", 0, 14),
+    ("EA", 1, 1),
+    ("XH", 0, 5),
+    ("TA", 0, 0),
+    ("SQ", 1, 4),
 )
-X_HAT_ON_VECTOR = [26,27,28,29,30,31]
+X_HAT_ON_VECTOR = [6,7,10,12,15,17,19,20,22,23,24,25,26,28,29,30,31]
+INTERLEAVE_ON_VECTOR = [10,11,12,13,14]
+RELU_ON_SCALAR = [0,1,3,4,5,7,8,9,10,11,12,13]
 
 
 def tile_rotaryembeddingtransformerlayer_pb_t_w4_kernel(
@@ -76,10 +77,8 @@ def tile_rotaryembeddingtransformerlayer_pb_t_w4_kernel(
         psum = ctx.enter_context(tc.psum_pool(name="psum", bufs=1))
         ctx.enter_context(tc.manual_schedule())
 
-        warm = const.tile([P, 1], F32)
-        nc.vector.memset(warm[:], 0.0)
-        scale = const.tile([P, E], F32)
-        nc.scalar.dma_start(out=scale[:], in_=attn_scale.rearrange("a b k -> (a b k)").partition_broadcast(P))
+        scale = const.tile([P, 2 * E], F32)
+        scale_row = attn_scale.rearrange("a b k -> (a b k)")
         byte_tiles = [const.tile([P, 2 * E], U8, name="bytes%d" % n) for n in range(PAIRS)]
         src_tiles = [const.tile([P, 4 * D], BF16, name="src%d" % n) for n in range(PAIRS // 2)]
         wo = const.tile([P, 2, 2 * D], U8, align_bytes=64)
@@ -92,17 +91,20 @@ def tile_rotaryembeddingtransformerlayer_pb_t_w4_kernel(
         be2_raw = const.tile([P, 4], BF16)
         g2_col = const.tile([P, 4], F32)
         be2_col = const.tile([P, 4], F32)
-        half = const.tile([P, 2], F32)
+        eps = const.tile([P, 1], F32)
+        warm = const.tile([P, 1], F32)
         identity = const.tile([P, P], F32)
 
         def load_bytes(n):
             nc.sync.dma_start(out=byte_tiles[n][:], in_=bytes_in[n // 2][:, (n % 2) * 2 * E : (n % 2 + 1) * 2 * E])
 
+        for k0 in (0, E // 2):
+            nc.scalar.dma_start(out=scale[:, k0 : k0 + E // 2], in_=scale_row[k0 : k0 + E // 2].partition_broadcast(P))
+        load_bytes(0)
+        nc.gpsimd.memset(eps[:], EPS)
         nc.vector.memset(wo_s[:].rearrange("p g n -> p (g n)").bitcast(I32), 0)
         nc.vector.memset(w1_s[:].bitcast(I32), 0)
-        nc.gpsimd.memset(half[:], -0.5)
-        load_bytes(0)
-        nc.scalar.activation(out=warm[:], in_=warm[:], func=SQUARE)
+        nc.scalar.activation(out=warm[:], in_=eps[:], func=ARS, bias=eps[:])
         make_identity(nc, identity[:])
         load_bytes(1)
         nc.sync.dma_start(out=wo[:], in_=Wo_words.rearrange("g p b -> p g b"))
@@ -128,22 +130,31 @@ def tile_rotaryembeddingtransformerlayer_pb_t_w4_kernel(
             load_bytes(n)
             load_bytes(n + 1)
         nc.sync.dma_start(out=src_tiles[PAIRS // 2 - 1][:], in_=src_in[PAIRS // 2 - 1])
+        nc.scalar.copy(out=scale[:, E : 2 * E], in_=scale[:, 0:E])
         nc.gpsimd.tensor_copy(out=g2_col[:], in_=g2_raw[:])
         nc.gpsimd.tensor_copy(out=be2_col[:], in_=be2_raw[:])
 
         t = {}
 
         def product(n, i):
-            a = work.tile([P, E], BF16, name="a", tag="a", bufs=4)
-            t["a", n, i] = a
-            nc.vector.tensor_tensor(
-                out=a[:], in0=byte_tiles[n][:, i * E : (i + 1) * E].bitcast(FP8), in1=scale[:], op=MULT
-            )
+            if n == 0:
+                if i == 0:
+                    t["a", 0] = work.tile([P, 2 * E], BF16, name="a", tag="a", bufs=3)
+                for k0 in range(i * E, (i + 1) * E, E // 2):
+                    nc.vector.tensor_tensor(
+                        out=t["a", 0][:, k0 : k0 + E // 2],
+                        in0=byte_tiles[0][:, k0 : k0 + E // 2].bitcast(FP8),
+                        in1=scale[:, k0 % E : k0 % E + E // 2],
+                        op=MULT,
+                    )
+            elif i == 0:
+                t["a", n] = work.tile([P, 2 * E], BF16, name="a", tag="a", bufs=3)
+                nc.vector.tensor_tensor(out=t["a", n][:], in0=byte_tiles[n][:].bitcast(FP8), in1=scale[:], op=MULT)
 
         def turn_a(n, i):
             at = psum.tile([P, 2, 2, P], F32, name="at", tag="at", bufs=2)
             t["at", n, i] = at
-            words = t["a", n, i][:].bitcast(F32)
+            words = t["a", n][:, i * E : (i + 1) * E].bitcast(F32)
             for g in range(2):
                 for j in range(2):
                     nc.tensor.transpose(at[:, g, j, :], words[:, 256 * g + j : 256 * (g + 1) : 2], identity[:])
@@ -166,7 +177,7 @@ def tile_rotaryembeddingtransformerlayer_pb_t_w4_kernel(
             )
 
         def multiply_a(n, i):
-            y = psum.tile([P, D], F32, name="y", tag="y", bufs=3)
+            y = psum.tile([P, D], F32, name="y", tag="y", bufs=4)
             t["y", n, i] = y
             for g in range(2):
                 cols = slice((2 * i + g) * P, (2 * i + g + 1) * P)
@@ -181,22 +192,21 @@ def tile_rotaryembeddingtransformerlayer_pb_t_w4_kernel(
                 )
 
         def add_bias(n, i):
-            sb = work.tile([P, 2, D], F32, name="sb", tag="sb", bufs=3)
-            t["sb", n] = sb
+            t["sb", n] = work.tile([P, 2, D], F32, name="sb", tag="sb", bufs=3)
+            d0 = n % 2 * 2 * D
             nc.vector.tensor_tensor(
-                out=sb[:],
-                in0=src_tiles[n // 2][:, (n % 2) * 2 * D : (n % 2 + 1) * 2 * D].rearrange("p (r d) -> p r d", r=2),
+                out=t["sb", n][:],
+                in0=src_tiles[n // 2][:, d0 : d0 + 2 * D].rearrange("p (r d) -> p r d", d=D),
                 in1=bo_row[:].unsqueeze(1).to_broadcast([P, 2, D]),
                 op=ADD,
             )
 
         def add_x(n, i):
-            if ("x", n) not in t:
-                t["x", n] = work.tile([P, 2, D], F32, name="x", tag="x", bufs=5)
-                t["sum", n] = work.tile([P, 2], F32, name="sum_", tag="sum", bufs=4)
-                t["nm", n] = work.tile([P, 2], F32, name="nm", tag="nm", bufs=4)
-                t["sq", n] = work.tile([P, 2], F32, name="sq", tag="sq", bufs=4)
-                t["st", n] = work.tile([P, 3, 2], F32, name="st", tag="st", bufs=4)
+            other_done = ("x", n) in t
+            if not other_done:
+                t["x", n] = work.tile([P, 2, D], F32, name="x", tag="x", bufs=6)
+                for name in ("sum", "nm", "sq", "rs", "nr"):
+                    t[name, n] = work.tile([P, 2], F32, name=name, tag=name, bufs=6)
             nc.vector.scalar_tensor_tensor(
                 out=t["x", n][:, i, :],
                 in0=t["y", n, i][:],
@@ -206,15 +216,12 @@ def tile_rotaryembeddingtransformerlayer_pb_t_w4_kernel(
                 op1=ADD,
                 accum_out=t["sum", n][:, i : i + 1],
             )
-            if ("xdone", n) in t:
-                nc.gpsimd.tensor_scalar(
-                    out=t["nm", n][:], in0=t["sum", n][:], scalar1=-1.0 / D, scalar2=0.0, op0=MULT, op1=ADD
-                )
-                nc.sync.dma_start(
-                    out=x_hbm[n // 2][:, (n % 2) * 2 * D : (n % 2 + 1) * 2 * D],
-                    in_=t["x", n][:].rearrange("p r d -> p (r d)"),
-                )
-            t["xdone", n] = True
+            if other_done:
+                d0 = n % 2 * 2 * D
+                nc.sync.dma_start(out=x_hbm[n // 2][:, d0 : d0 + 2 * D], in_=t["x", n][:].rearrange("p r d -> p (r d)"))
+
+        def negative_mean(n, i):
+            nc.gpsimd.tensor_scalar(out=t["nm", n][:], in0=t["sum", n][:], scalar1=-1.0 / D, scalar2=None, op0=MULT)
 
         def square(n, i):
             junk = work.tile([P, D], BF16, name="junk", tag="junk", bufs=2)
@@ -222,40 +229,38 @@ def tile_rotaryembeddingtransformerlayer_pb_t_w4_kernel(
                 out=junk[:],
                 in_=t["x", n][:, i, :],
                 func=SQUARE,
-                bias=t["nm", n][:, i : i + 1],
+                scale=-float(D),
+                bias=t["sum", n][:, i : i + 1],
                 accum_out=t["sq", n][:, i : i + 1],
             )
-            if ("sqdone", n) in t:
-                st = t["st", n]
-                nc.gpsimd.tensor_scalar(
-                    out=st[:, 0, :], in0=t["sq", n][:], scalar1=1.0 / D, scalar2=EPS, op0=MULT, op1=ADD
-                )
-                nc.gpsimd.tensor_tensor(out=st[:, 1, :], in0=st[:, 0, :], in1=half[:], op=POW)
-                nc.gpsimd.tensor_tensor(out=st[:, 2, :], in0=t["nm", n][:], in1=st[:, 1, :], op=MULT)
-            t["sqdone", n] = True
+
+        def inverse_std(n, i):
+            nc.scalar.activation(out=t["rs", n][:], in_=t["sq", n][:], func=ARS, scale=1.0 / D**3, bias=eps[:])
+
+        def scaled_mean(n, i):
+            if not (2 * n in X_HAT_ON_VECTOR and 2 * n + 1 in X_HAT_ON_VECTOR):
+                nc.gpsimd.tensor_tensor(out=t["nr", n][:], in0=t["nm", n][:], in1=t["rs", n][:], op=MULT)
 
         def normalise(n, i):
-            xh = work.tile([P, 4, P], F32, name="xh", tag="xh", bufs=4)
+            xh = work.tile([P, 4, P], F32, name="xh", tag="xh", bufs=6)
             t["xh", n, i] = xh
             x = t["x", n][:, i, :].rearrange("p (m t) -> p t m", t=4)
-            st = t["st", n]
+            rs = t["rs", n][:, i : i + 1]
             if 2 * n + i in X_HAT_ON_VECTOR:
-                nc.vector.tensor_scalar(
-                    out=xh[:], in0=x, scalar1=t["nm", n][:, i : i + 1], scalar2=st[:, 1, i : i + 1], op0=ADD, op1=MULT
-                )
+                nc.vector.tensor_scalar(out=xh[:], in0=x, scalar1=t["nm", n][:, i : i + 1], scalar2=rs, op0=ADD, op1=MULT)
             else:
-                nc.scalar.activation(out=xh[:], in_=x, func=IDENT, scale=st[:, 1, i : i + 1], bias=st[:, 2, i : i + 1])
+                nc.scalar.activation(out=xh[:], in_=x, func=IDENT, scale=rs, bias=t["nr", n][:, i : i + 1])
 
-        def turn_h(n, i):
-            if ("ht", n, 0) not in t:
-                for b in range(2):
-                    t["ht", n, b] = psum.tile([P, 2, 2, P], F32, name="ht", tag="ht", bufs=2)
-            for c in range(4):
-                nc.tensor.transpose(t["ht", n, c // 2][:, c % 2, i, :], t["xh", n, i][:, c, :], identity[:])
+        def turn_h(n, h):
+            ht = psum.tile([P, 2, 2, P], F32, name="ht", tag="ht", bufs=2)
+            t["ht", n, h] = ht
+            for c in range(2):
+                for i in range(2):
+                    nc.tensor.transpose(ht[:, c, i, :], t["xh", n, i][:, 2 * h + c, :], identity[:])
 
         def empty_h(n, c):
             if ("hp", n) not in t:
-                t["hp", n] = work.tile([P, 4, 256], BF16, name="hp", tag="hp", bufs=4)
+                t["hp", n] = work.tile([P, 4, 2 * P], BF16, name="hp", tag="hp", bufs=5)
             nc.scalar.activation(
                 out=t["hp", n][:, c, :],
                 in_=t["ht", n, c // 2][:, c % 2, :, :].rearrange("p i r -> p (i r)"),
@@ -265,20 +270,20 @@ def tile_rotaryembeddingtransformerlayer_pb_t_w4_kernel(
             )
 
         def interleave(n, i):
-            if ("hg", n) not in t:
-                t["hg", n] = work.tile([P, 1024], BF16, name="hg", tag="hg", bufs=3, align_bytes=64)
-            nc.scalar.copy(
-                out=t["hg", n][:, i * 512 : (i + 1) * 512].rearrange("p (c s t) -> p c t s", s=4, t=4),
-                in_=t["hp", n][:, :, i * P : (i + 1) * P].rearrange("p t (c s) -> p c t s", s=4),
+            t["hg", n] = work.tile([P, 8 * P], BF16, name="hg", tag="hg", bufs=4, align_bytes=64)
+            copy = nc.vector.tensor_copy if n in INTERLEAVE_ON_VECTOR else nc.scalar.copy
+            copy(
+                out=t["hg", n][:].rearrange("p (c s t) -> p c t s", s=4, t=4),
+                in_=t["hp", n][:].rearrange("p t (c s) -> p c t s", s=4),
             )
 
         def quantise_h(n, i):
-            t["hc", n] = work.tile([P, 256], U32, name="hc", tag="hc", bufs=3, align_bytes=64)
-            t["hs", n] = work.tile([P, 256], U8, name="hs", tag="hs", bufs=3, align_bytes=64)
+            t["hc", n] = work.tile([P, 2 * P], U32, name="hc", tag="hc", bufs=4, align_bytes=64)
+            t["hs", n] = work.tile([P, 2 * P], U8, name="hs", tag="hs", bufs=4, align_bytes=64)
             nc.vector.quantize_mx(out=t["hc", n][:].bitcast(FP8X4), scales=t["hs", n][:], in_=t["hg", n][:])
 
         def multiply_h(n, i):
-            up = psum.tile([P, 2, F], F32, name="up", tag="up", bufs=1)
+            up = psum.tile([P, 2, F], F32, name="up", tag="y", bufs=4)
             t["up", n] = up
             for r in range(2):
                 cols = slice(r * P, (r + 1) * P)
@@ -293,28 +298,26 @@ def tile_rotaryembeddingtransformerlayer_pb_t_w4_kernel(
                 )
 
         def add_u(n, i):
-            us = work.tile([P, 2, F], F32, name="us", tag="us", bufs=4)
-            t["us", n] = us
+            t["us", n] = work.tile([P, 2, F], F32, name="us", tag="us", bufs=4)
             nc.vector.tensor_tensor(
-                out=us[:], in0=t["up", n][:], in1=b1_row[:].unsqueeze(1).to_broadcast([P, 2, F]), op=ADD
+                out=t["us", n][:], in0=t["up", n][:], in1=b1_row[:].unsqueeze(1).to_broadcast([P, 2, F]), op=ADD
             )
 
         def relu_u(n, i):
-            uo = work.tile([P, 2, F], F32, name="uo", tag="uo", bufs=3)
+            uo = work.tile([P, 2, F], F32, name="uo", tag="uo", bufs=4)
             if n in RELU_ON_SCALAR:
                 nc.scalar.activation(out=uo[:], in_=t["us", n][:], func=RELU)
             else:
                 nc.vector.tensor_scalar(out=uo[:], in0=t["us", n][:], scalar1=0.0, scalar2=None, op0=MAX)
-            nc.sync.dma_start(
-                out=u_hbm[n // 2][:, (n % 2) * 2 * F : (n % 2 + 1) * 2 * F], in_=uo[:].rearrange("p r f -> p (r f)")
-            )
+            f0 = n % 2 * 2 * F
+            nc.sync.dma_start(out=u_hbm[n // 2][:, f0 : f0 + 2 * F], in_=uo[:].rearrange("p r f -> p (r f)"))
 
         stages = {
             "P": product, "TA": turn_a, "EA": empty_a, "QA": quantise_a, "MM": multiply_a, "SB": add_bias,
-            "XA": add_x, "SQ": square, "XH": normalise, "TH": turn_h, "EH": empty_h, "IL": interleave,
-            "QB": quantise_h, "M2": multiply_h, "UA": add_u, "RL": relu_u,
+            "XA": add_x, "NM": negative_mean, "SQ": square, "AR": inverse_std, "NR": scaled_mean, "XH": normalise,
+            "TH": turn_h, "EH": empty_h, "IL": interleave, "QB": quantise_h, "M2": multiply_h, "UA": add_u, "RL": relu_u,
         }
-        for s in range(PAIRS + max(lag for a, b, lag in SLOT)):
+        for s in range(PAIRS + max(lag for name, i, lag in SLOT)):
             for name, i, lag in SLOT:
                 if 0 <= s - lag < PAIRS:
                     stages[name](s - lag, i)

@@ -22,44 +22,45 @@ ARS = mybir.ActivationFunctionType.Abs_reciprocal_sqrt
 P = 128
 TOKENS, D, E, F = 4096, 512, 1024, 256
 PAIRS = TOKENS // 256
+SMALL = (("bo", 4), ("b1", 2), ("g2", 4), ("be2", 4))
 EPS = 1e-5
 FLOPS = 2 * TOKENS * (E * D + D * F)
 
 SLOT = (
-    ("XA", 1, 4),
-    ("SQ", 0, 5),
-    ("TA", 1, 1),
-    ("XA", 0, 4),
-    ("MM", 1, 3),
-    ("MM", 0, 3),
-    ("EH", 2, 7),
-    ("AR", 0, 5),
-    ("EH", 3, 7),
-    ("M2", 0, 13),
-    ("XH", 1, 6),
-    ("QB", 0, 11),
-    ("NM", 0, 5),
-    ("P", 0, 0),
-    ("IL", 0, 9),
-    ("EH", 1, 7),
-    ("EH", 0, 7),
-    ("NR", 0, 5),
+    ("AR", 0, 4),
     ("TH", 1, 6),
-    ("SB", 0, 3),
-    ("RL", 0, 16),
-    ("TH", 0, 6),
     ("QA", 0, 2),
-    ("P", 1, 0),
-    ("EA", 0, 1),
-    ("UA", 0, 14),
-    ("EA", 1, 1),
+    ("IL", 0, 8),
+    ("RL", 0, 14),
+    ("NM", 0, 3),
+    ("EH", 1, 6),
+    ("TA", 0, 1),
+    ("TA", 1, 1),
+    ("EH", 0, 6),
+    ("EH", 3, 6),
+    ("SQ", 0, 3),
     ("XH", 0, 5),
-    ("TA", 0, 0),
-    ("SQ", 1, 4),
+    ("XH", 1, 5),
+    ("P", 0, 0),
+    ("MM", 0, 2),
+    ("MM", 1, 2),
+    ("UA", 0, 12),
+    ("M2", 0, 11),
+    ("TH", 0, 5),
+    ("QB", 0, 9),
+    ("XA", 0, 2),
+    ("XA", 1, 2),
+    ("EA", 0, 1),
+    ("EA", 1, 1),
+    ("SB", 0, 1),
+    ("P", 1, 0),
+    ("SQ", 1, 3),
+    ("EH", 2, 6),
+    ("NR", 0, 4),
 )
-X_HAT_ON_VECTOR = [6,7,10,12,15,17,19,20,22,23,24,25,26,28,29,30,31]
-INTERLEAVE_ON_VECTOR = [10,11,12,13,14]
-RELU_ON_SCALAR = [0,1,3,4,5,7,8,9,10,11,12,13]
+X_HAT_ON_VECTOR = [5,12,16,22,24,25,26,27,28,29,30,31]
+INTERLEAVE_ON_VECTOR = [8,11,13,14]
+RELU_ON_SCALAR = [0,4,7,9,10,11,12,13]
 
 
 def tile_rotaryembeddingtransformerlayer_pb_t_w4_kernel(
@@ -78,7 +79,6 @@ def tile_rotaryembeddingtransformerlayer_pb_t_w4_kernel(
         ctx.enter_context(tc.manual_schedule())
 
         scale = const.tile([P, 2 * E], F32)
-        scale_row = attn_scale.rearrange("a b k -> (a b k)")
         byte_tiles = [const.tile([P, 2 * E], U8, name="bytes%d" % n) for n in range(PAIRS)]
         src_tiles = [const.tile([P, 4 * D], BF16, name="src%d" % n) for n in range(PAIRS // 2)]
         wo = const.tile([P, 2, 2 * D], U8, align_bytes=64)
@@ -87,10 +87,9 @@ def tile_rotaryembeddingtransformerlayer_pb_t_w4_kernel(
         w1_s = const.tile([P, F], U8, align_bytes=64)
         bo_row = const.tile([P, D], BF16)
         b1_row = const.tile([P, F], BF16)
-        g2_raw = const.tile([P, 4], BF16)
-        be2_raw = const.tile([P, 4], BF16)
-        g2_col = const.tile([P, 4], F32)
-        be2_col = const.tile([P, 4], F32)
+        scale_raw = const.tile([P, 2, 4], F32)
+        raw = {name: const.tile([P, width], BF16, name=name + "_raw") for name, width in SMALL}
+        col = {name: const.tile([P, width], F32, name=name + "_col") for name, width in SMALL}
         eps = const.tile([P, 1], F32)
         warm = const.tile([P, 1], F32)
         identity = const.tile([P, P], F32)
@@ -98,26 +97,23 @@ def tile_rotaryembeddingtransformerlayer_pb_t_w4_kernel(
         def load_bytes(n):
             nc.sync.dma_start(out=byte_tiles[n][:], in_=bytes_in[n // 2][:, (n % 2) * 2 * E : (n % 2 + 1) * 2 * E])
 
-        for k0 in (0, E // 2):
-            nc.scalar.dma_start(out=scale[:, k0 : k0 + E // 2], in_=scale_row[k0 : k0 + E // 2].partition_broadcast(P))
+        nc.scalar.dma_start(out=scale_raw[:], in_=attn_scale.rearrange("a b (h p c) -> p (a b h) c", h=2, c=4))
+        for vector, (name, width) in zip((bo, b1, g2, be2), SMALL):
+            nc.scalar.dma_start(out=raw[name][:], in_=vector.rearrange("(p c) -> p c", c=width))
         load_bytes(0)
         nc.gpsimd.memset(eps[:], EPS)
+        make_identity(nc, identity[:])
         nc.vector.memset(wo_s[:].rearrange("p g n -> p (g n)").bitcast(I32), 0)
         nc.vector.memset(w1_s[:].bitcast(I32), 0)
         nc.scalar.activation(out=warm[:], in_=eps[:], func=ARS, bias=eps[:])
-        make_identity(nc, identity[:])
-        load_bytes(1)
         nc.sync.dma_start(out=wo[:], in_=Wo_words.rearrange("g p b -> p g b"))
         for Q in range(4):
             nc.sync.dma_start(
                 out=wo_s[32 * Q : 32 * Q + 4].bitcast(I32),
                 in_=Wo_scales[:, 4 * Q : 4 * Q + 4, :].rearrange("g q n -> q g n").bitcast(I32),
             )
-        nc.scalar.dma_start(out=bo_row[:], in_=bo.partition_broadcast(P))
+        load_bytes(1)
         nc.sync.dma_start(out=src_tiles[0][:], in_=src_in[0])
-        nc.scalar.dma_start(out=g2_raw[:], in_=g2.rearrange("(p t) -> p t", t=4))
-        nc.scalar.dma_start(out=be2_raw[:], in_=be2.rearrange("(p t) -> p t", t=4))
-        nc.scalar.dma_start(out=b1_row[:], in_=b1.partition_broadcast(P))
         load_bytes(2)
         load_bytes(3)
         nc.sync.dma_start(out=w1[:], in_=W1_words[0])
@@ -130,25 +126,38 @@ def tile_rotaryembeddingtransformerlayer_pb_t_w4_kernel(
             load_bytes(n)
             load_bytes(n + 1)
         nc.sync.dma_start(out=src_tiles[PAIRS // 2 - 1][:], in_=src_in[PAIRS // 2 - 1])
-        nc.scalar.copy(out=scale[:, E : 2 * E], in_=scale[:, 0:E])
-        nc.gpsimd.tensor_copy(out=g2_col[:], in_=g2_raw[:])
-        nc.gpsimd.tensor_copy(out=be2_col[:], in_=be2_raw[:])
+
+        def spread(row, columns, tag, bufs, copy):
+            width = columns.shape[1]
+            bank = psum.tile([P, 4, P], F32, name=tag, tag=tag, bufs=bufs)
+            for c in range(width):
+                nc.tensor.transpose(bank[:, c, :], columns[:, c : c + 1].to_broadcast([P, P]), identity[:])
+            copy(out=row.rearrange("p (q c) -> p q c", c=width), in_=bank[:, 0:width, :].rearrange("p c q -> p q c"))
+
+        for h, copy in enumerate((nc.scalar.copy, nc.vector.tensor_copy)):
+            spread(scale[:, h * E // 2 : (h + 1) * E // 2], scale_raw[:, h, :], "at", 2, copy)
+        for name, width in SMALL:
+            nc.scalar.copy(out=col[name][:], in_=raw[name][:])
+        spread(bo_row[:], col["bo"][:], "ht", 3, nc.scalar.copy)
+        spread(b1_row[:], col["b1"][:], "ht", 3, nc.scalar.copy)
 
         t = {}
 
         def product(n, i):
-            if n == 0:
-                if i == 0:
-                    t["a", 0] = work.tile([P, 2 * E], BF16, name="a", tag="a", bufs=3)
-                for k0 in range(i * E, (i + 1) * E, E // 2):
+            if i == 0:
+                t["a", n] = work.tile([P, 2 * E], BF16, name="a", tag="a", bufs=3)
+            if n < 2:
+                step = E // 2 if n == 0 else E
+                for k0 in range(i * E, (i + 1) * E, step):
                     nc.vector.tensor_tensor(
-                        out=t["a", 0][:, k0 : k0 + E // 2],
-                        in0=byte_tiles[0][:, k0 : k0 + E // 2].bitcast(FP8),
-                        in1=scale[:, k0 % E : k0 % E + E // 2],
+                        out=t["a", n][:, k0 : k0 + step],
+                        in0=byte_tiles[n][:, k0 : k0 + step].bitcast(FP8),
+                        in1=scale[:, k0 % E : k0 % E + step],
                         op=MULT,
                     )
+                if n == 1 and i == 0:
+                    nc.scalar.copy(out=scale[:, E : 2 * E], in_=scale[:, 0:E])
             elif i == 0:
-                t["a", n] = work.tile([P, 2 * E], BF16, name="a", tag="a", bufs=3)
                 nc.vector.tensor_tensor(out=t["a", n][:], in0=byte_tiles[n][:].bitcast(FP8), in1=scale[:], op=MULT)
 
         def turn_a(n, i):
@@ -177,7 +186,7 @@ def tile_rotaryembeddingtransformerlayer_pb_t_w4_kernel(
             )
 
         def multiply_a(n, i):
-            y = psum.tile([P, D], F32, name="y", tag="y", bufs=4)
+            y = psum.tile([P, D], F32, name="y", tag="y", bufs=3)
             t["y", n, i] = y
             for g in range(2):
                 cols = slice((2 * i + g) * P, (2 * i + g + 1) * P)
@@ -252,7 +261,7 @@ def tile_rotaryembeddingtransformerlayer_pb_t_w4_kernel(
                 nc.scalar.activation(out=xh[:], in_=x, func=IDENT, scale=rs, bias=t["nr", n][:, i : i + 1])
 
         def turn_h(n, h):
-            ht = psum.tile([P, 2, 2, P], F32, name="ht", tag="ht", bufs=2)
+            ht = psum.tile([P, 2, 2, P], F32, name="ht", tag="ht", bufs=3)
             t["ht", n, h] = ht
             for c in range(2):
                 for i in range(2):
@@ -260,13 +269,13 @@ def tile_rotaryembeddingtransformerlayer_pb_t_w4_kernel(
 
         def empty_h(n, c):
             if ("hp", n) not in t:
-                t["hp", n] = work.tile([P, 4, 2 * P], BF16, name="hp", tag="hp", bufs=5)
+                t["hp", n] = work.tile([P, 4, 2 * P], BF16, name="hp", tag="hp", bufs=4)
             nc.scalar.activation(
                 out=t["hp", n][:, c, :],
                 in_=t["ht", n, c // 2][:, c % 2, :, :].rearrange("p i r -> p (i r)"),
                 func=IDENT,
-                scale=g2_col[:, c : c + 1],
-                bias=be2_col[:, c : c + 1],
+                scale=col["g2"][:, c : c + 1],
+                bias=col["be2"][:, c : c + 1],
             )
 
         def interleave(n, i):
@@ -283,7 +292,7 @@ def tile_rotaryembeddingtransformerlayer_pb_t_w4_kernel(
             nc.vector.quantize_mx(out=t["hc", n][:].bitcast(FP8X4), scales=t["hs", n][:], in_=t["hg", n][:])
 
         def multiply_h(n, i):
-            up = psum.tile([P, 2, F], F32, name="up", tag="y", bufs=4)
+            up = psum.tile([P, 2, F], F32, name="up", tag="y", bufs=3)
             t["up", n] = up
             for r in range(2):
                 cols = slice(r * P, (r + 1) * P)

from contextlib import ExitStack

import concourse.mybir as mybir
from concourse.masks import make_identity

F32 = mybir.dt.float32
BF16 = mybir.dt.bfloat16
U8 = mybir.dt.uint8
U32 = mybir.dt.uint32
I32 = mybir.dt.int32
FP8 = mybir.dt.float8_e4m3fn
FP8X4 = mybir.dt.float8_e4m3fn_x4
FP4X4 = mybir.dt.float4_e2m1fn_x4
ADD = mybir.AluOpType.add
MULT = mybir.AluOpType.mult
MAX = mybir.AluOpType.max
IDENT = mybir.ActivationFunctionType.Identity
SQUARE = mybir.ActivationFunctionType.Square
RELU = mybir.ActivationFunctionType.Relu
ARS = mybir.ActivationFunctionType.Abs_reciprocal_sqrt

P = 128
TOKENS, D, E, F = 4096, 512, 1024, 256
PAIRS = TOKENS // 256
SMALL = (("bo", 4), ("b1", 2), ("g2", 4), ("be2", 4))
EPS = 1e-5
FLOPS = 2 * TOKENS * (E * D + D * F)

SLOT = (
    ("AR", 0, 4),
    ("TH", 1, 6),
    ("QA", 0, 2),
    ("IL", 0, 8),
    ("RL", 0, 14),
    ("NM", 0, 3),
    ("EH", 1, 6),
    ("TA", 0, 1),
    ("TA", 1, 1),
    ("EH", 0, 6),
    ("EH", 3, 6),
    ("SQ", 0, 3),
    ("XH", 0, 5),
    ("XH", 1, 5),
    ("P", 0, 0),
    ("MM", 0, 2),
    ("MM", 1, 2),
    ("UA", 0, 12),
    ("M2", 0, 11),
    ("TH", 0, 5),
    ("QB", 0, 9),
    ("XA", 0, 2),
    ("XA", 1, 2),
    ("EA", 0, 1),
    ("EA", 1, 1),
    ("SB", 0, 1),
    ("P", 1, 0),
    ("SQ", 1, 3),
    ("EH", 2, 6),
    ("NR", 0, 4),
)
X_HAT_ON_VECTOR = [5,12,16,22,24,25,26,27,28,29,30,31]
INTERLEAVE_ON_VECTOR = [8,11,13,14]
RELU_ON_SCALAR = [0,4,7,9,10,11,12,13]


def tile_rotaryembeddingtransformerlayer_pb_t_w4_kernel(
    tc, attn_bytes, attn_scale, src_norm, Wo_words, Wo_scales, bo, g2, be2, W1_words, W1_scales, b1, x_out, u_out
):
    nc = tc.nc
    bytes_in = attn_bytes.flatten_outer_dims().rearrange("(q p r) k -> q p (r k)", p=P, r=4)
    src_in = src_norm.flatten_outer_dims().rearrange("(q p r) d -> q p (r d)", p=P, r=4)
    x_hbm = x_out.flatten_outer_dims().rearrange("(q p r) d -> q p (r d)", p=P, r=4)
    u_hbm = u_out.flatten_outer_dims().rearrange("(q p r) f -> q p (r f)", p=P, r=4)

    with ExitStack() as ctx:
        const = ctx.enter_context(tc.tile_pool(name="const", bufs=1))
        work = ctx.enter_context(tc.tile_pool(name="work", bufs=2))
        psum = ctx.enter_context(tc.psum_pool(name="psum", bufs=1))
        ctx.enter_context(tc.manual_schedule())

        scale = const.tile([P, 2 * E], F32)
        byte_tiles = [const.tile([P, 2 * E], U8, name="bytes%d" % n) for n in range(PAIRS)]
        src_tiles = [const.tile([P, 4 * D], BF16, name="src%d" % n) for n in range(PAIRS // 2)]
        wo = const.tile([P, 2, 2 * D], U8, align_bytes=64)
        wo_s = const.tile([P, 2, D], U8, align_bytes=64)
        w1 = const.tile([P, 2 * F], U8, align_bytes=64)
        w1_s = const.tile([P, F], U8, align_bytes=64)
        bo_row = const.tile([P, D], BF16)
        b1_row = const.tile([P, F], BF16)
        scale_raw = const.tile([P, 2, 4], F32)
        raw = {name: const.tile([P, width], BF16, name=name + "_raw") for name, width in SMALL}
        col = {name: const.tile([P, width], F32, name=name + "_col") for name, width in SMALL}
        eps = const.tile([P, 1], F32)
        warm = const.tile([P, 1], F32)
        identity = const.tile([P, P], F32)

        def load_bytes(n):
            nc.sync.dma_start(out=byte_tiles[n][:], in_=bytes_in[n // 2][:, (n % 2) * 2 * E : (n % 2 + 1) * 2 * E])

        nc.scalar.dma_start(out=scale_raw[:], in_=attn_scale.rearrange("a b (h p c) -> p (a b h) c", h=2, c=4))
        for vector, (name, width) in zip((bo, b1, g2, be2), SMALL):
            nc.scalar.dma_start(out=raw[name][:], in_=vector.rearrange("(p c) -> p c", c=width))
        load_bytes(0)
        nc.gpsimd.memset(eps[:], EPS)
        make_identity(nc, identity[:])
        nc.vector.memset(wo_s[:].rearrange("p g n -> p (g n)").bitcast(I32), 0)
        nc.vector.memset(w1_s[:].bitcast(I32), 0)
        nc.scalar.activation(out=warm[:], in_=eps[:], func=ARS, bias=eps[:])
        nc.sync.dma_start(out=wo[:], in_=Wo_words.rearrange("g p b -> p g b"))
        for Q in range(4):
            nc.sync.dma_start(
                out=wo_s[32 * Q : 32 * Q + 4].bitcast(I32),
                in_=Wo_scales[:, 4 * Q : 4 * Q + 4, :].rearrange("g q n -> q g n").bitcast(I32),
            )
        load_bytes(1)
        nc.sync.dma_start(out=src_tiles[0][:], in_=src_in[0])
        load_bytes(2)
        load_bytes(3)
        nc.sync.dma_start(out=w1[:], in_=W1_words[0])
        for Q in range(4):
            nc.sync.dma_start(
                out=w1_s[32 * Q : 32 * Q + 4].bitcast(I32), in_=W1_scales[0, 4 * Q : 4 * Q + 4, :].bitcast(I32)
            )
        for n in range(4, PAIRS, 2):
            nc.sync.dma_start(out=src_tiles[n // 2 - 1][:], in_=src_in[n // 2 - 1])
            load_bytes(n)
            load_bytes(n + 1)
        nc.sync.dma_start(out=src_tiles[PAIRS // 2 - 1][:], in_=src_in[PAIRS // 2 - 1])

        def spread(row, columns, tag, bufs, copy):
            width = columns.shape[1]
            bank = psum.tile([P, 4, P], F32, name=tag, tag=tag, bufs=bufs)
            for c in range(width):
                nc.tensor.transpose(bank[:, c, :], columns[:, c : c + 1].to_broadcast([P, P]), identity[:])
            copy(out=row.rearrange("p (q c) -> p q c", c=width), in_=bank[:, 0:width, :].rearrange("p c q -> p q c"))

        for h, copy in enumerate((nc.scalar.copy, nc.vector.tensor_copy)):
            spread(scale[:, h * E // 2 : (h + 1) * E // 2], scale_raw[:, h, :], "at", 2, copy)
        for name, width in SMALL:
            nc.scalar.copy(out=col[name][:], in_=raw[name][:])
        spread(bo_row[:], col["bo"][:], "ht", 3, nc.scalar.copy)
        spread(b1_row[:], col["b1"][:], "ht", 3, nc.scalar.copy)

        t = {}

        def product(n, i):
            if i == 0:
                t["a", n] = work.tile([P, 2 * E], BF16, name="a", tag="a", bufs=3)
            if n < 2:
                step = E // 2 if n == 0 else E
                for k0 in range(i * E, (i + 1) * E, step):
                    nc.vector.tensor_tensor(
                        out=t["a", n][:, k0 : k0 + step],
                        in0=byte_tiles[n][:, k0 : k0 + step].bitcast(FP8),
                        in1=scale[:, k0 % E : k0 % E + step],
                        op=MULT,
                    )
                if n == 1 and i == 0:
                    nc.scalar.copy(out=scale[:, E : 2 * E], in_=scale[:, 0:E])
            elif i == 0:
                nc.vector.tensor_tensor(out=t["a", n][:], in0=byte_tiles[n][:].bitcast(FP8), in1=scale[:], op=MULT)

        def turn_a(n, i):
            at = psum.tile([P, 2, 2, P], F32, name="at", tag="at", bufs=2)
            t["at", n, i] = at
            words = t["a", n][:, i * E : (i + 1) * E].bitcast(F32)
            for g in range(2):
                for j in range(2):
                    nc.tensor.transpose(at[:, g, j, :], words[:, 256 * g + j : 256 * (g + 1) : 2], identity[:])

        def empty_a(n, i):
            if ("ag", n) not in t:
                t["ag", n] = work.tile([P, 2, 512], F32, name="ag", tag="ag", bufs=3, align_bytes=64)
            nc.scalar.copy(
                out=t["ag", n][:, i, :].rearrange("p (g r u) -> p g r u", g=2, u=2),
                in_=t["at", n, i][:].rearrange("p g u r -> p g r u"),
            )

        def quantise_a(n, i):
            t["ac", n] = work.tile([P, 512], U32, name="ac", tag="ac", bufs=3, align_bytes=64)
            t["as", n] = work.tile([P, 512], U8, name="as_", tag="as", bufs=3, align_bytes=64)
            nc.vector.quantize_mx(
                out=t["ac", n][:].bitcast(FP8X4),
                scales=t["as", n][:],
                in_=t["ag", n][:].rearrange("p i w -> p (i w)").bitcast(BF16),
            )

        def multiply_a(n, i):
            y = psum.tile([P, D], F32, name="y", tag="y", bufs=3)
            t["y", n, i] = y
            for g in range(2):
                cols = slice((2 * i + g) * P, (2 * i + g + 1) * P)
                nc.tensor.matmul_mx(
                    out=y[:],
                    lhsT=t["ac", n][:, cols].bitcast(FP8X4),
                    lhsT_scale=t["as", n][:, cols],
                    rhs=wo[:, g, :].bitcast(FP4X4),
                    rhs_scale=wo_s[:, g, :],
                    start=(g == 0),
                    stop=(g == 1),
                )

        def add_bias(n, i):
            t["sb", n] = work.tile([P, 2, D], F32, name="sb", tag="sb", bufs=3)
            d0 = n % 2 * 2 * D
            nc.vector.tensor_tensor(
                out=t["sb", n][:],
                in0=src_tiles[n // 2][:, d0 : d0 + 2 * D].rearrange("p (r d) -> p r d", d=D),
                in1=bo_row[:].unsqueeze(1).to_broadcast([P, 2, D]),
                op=ADD,
            )

        def add_x(n, i):
            other_done = ("x", n) in t
            if not other_done:
                t["x", n] = work.tile([P, 2, D], F32, name="x", tag="x", bufs=6)
                for name in ("sum", "nm", "sq", "rs", "nr"):
                    t[name, n] = work.tile([P, 2], F32, name=name, tag=name, bufs=6)
            nc.vector.scalar_tensor_tensor(
                out=t["x", n][:, i, :],
                in0=t["y", n, i][:],
                scalar=1.0,
                in1=t["sb", n][:, i, :],
                op0=MULT,
                op1=ADD,
                accum_out=t["sum", n][:, i : i + 1],
            )
            if other_done:
                d0 = n % 2 * 2 * D
                nc.sync.dma_start(out=x_hbm[n // 2][:, d0 : d0 + 2 * D], in_=t["x", n][:].rearrange("p r d -> p (r d)"))

        def negative_mean(n, i):
            nc.gpsimd.tensor_scalar(out=t["nm", n][:], in0=t["sum", n][:], scalar1=-1.0 / D, scalar2=None, op0=MULT)

        def square(n, i):
            junk = work.tile([P, D], BF16, name="junk", tag="junk", bufs=2)
            nc.scalar.activation(
                out=junk[:],
                in_=t["x", n][:, i, :],
                func=SQUARE,
                scale=-float(D),
                bias=t["sum", n][:, i : i + 1],
                accum_out=t["sq", n][:, i : i + 1],
            )

        def inverse_std(n, i):
            nc.scalar.activation(out=t["rs", n][:], in_=t["sq", n][:], func=ARS, scale=1.0 / D**3, bias=eps[:])

        def scaled_mean(n, i):
            if not (2 * n in X_HAT_ON_VECTOR and 2 * n + 1 in X_HAT_ON_VECTOR):
                nc.gpsimd.tensor_tensor(out=t["nr", n][:], in0=t["nm", n][:], in1=t["rs", n][:], op=MULT)

        def normalise(n, i):
            xh = work.tile([P, 4, P], F32, name="xh", tag="xh", bufs=6)
            t["xh", n, i] = xh
            x = t["x", n][:, i, :].rearrange("p (m t) -> p t m", t=4)
            rs = t["rs", n][:, i : i + 1]
            if 2 * n + i in X_HAT_ON_VECTOR:
                nc.vector.tensor_scalar(out=xh[:], in0=x, scalar1=t["nm", n][:, i : i + 1], scalar2=rs, op0=ADD, op1=MULT)
            else:
                nc.scalar.activation(out=xh[:], in_=x, func=IDENT, scale=rs, bias=t["nr", n][:, i : i + 1])

        def turn_h(n, h):
            ht = psum.tile([P, 2, 2, P], F32, name="ht", tag="ht", bufs=3)
            t["ht", n, h] = ht
            for c in range(2):
                for i in range(2):
                    nc.tensor.transpose(ht[:, c, i, :], t["xh", n, i][:, 2 * h + c, :], identity[:])

        def empty_h(n, c):
            if ("hp", n) not in t:
                t["hp", n] = work.tile([P, 4, 2 * P], BF16, name="hp", tag="hp", bufs=4)
            nc.scalar.activation(
                out=t["hp", n][:, c, :],
                in_=t["ht", n, c // 2][:, c % 2, :, :].rearrange("p i r -> p (i r)"),
                func=IDENT,
                scale=col["g2"][:, c : c + 1],
                bias=col["be2"][:, c : c + 1],
            )

        def interleave(n, i):
            t["hg", n] = work.tile([P, 8 * P], BF16, name="hg", tag="hg", bufs=4, align_bytes=64)
            copy = nc.vector.tensor_copy if n in INTERLEAVE_ON_VECTOR else nc.scalar.copy
            copy(
                out=t["hg", n][:].rearrange("p (c s t) -> p c t s", s=4, t=4),
                in_=t["hp", n][:].rearrange("p t (c s) -> p c t s", s=4),
            )

        def quantise_h(n, i):
            t["hc", n] = work.tile([P, 2 * P], U32, name="hc", tag="hc", bufs=4, align_bytes=64)
            t["hs", n] = work.tile([P, 2 * P], U8, name="hs", tag="hs", bufs=4, align_bytes=64)
            nc.vector.quantize_mx(out=t["hc", n][:].bitcast(FP8X4), scales=t["hs", n][:], in_=t["hg", n][:])

        def multiply_h(n, i):
            up = psum.tile([P, 2, F], F32, name="up", tag="y", bufs=3)
            t["up", n] = up
            for r in range(2):
                cols = slice(r * P, (r + 1) * P)
                nc.tensor.matmul_mx(
                    out=up[:, r, :],
                    lhsT=t["hc", n][:, cols].bitcast(FP8X4),
                    lhsT_scale=t["hs", n][:, cols],
                    rhs=w1[:].bitcast(FP4X4),
                    rhs_scale=w1_s[:],
                    start=True,
                    stop=True,
                )

        def add_u(n, i):
            t["us", n] = work.tile([P, 2, F], F32, name="us", tag="us", bufs=4)
            nc.vector.tensor_tensor(
                out=t["us", n][:], in0=t["up", n][:], in1=b1_row[:].unsqueeze(1).to_broadcast([P, 2, F]), op=ADD
            )

        def relu_u(n, i):
            uo = work.tile([P, 2, F], F32, name="uo", tag="uo", bufs=4)
            if n in RELU_ON_SCALAR:
                nc.scalar.activation(out=uo[:], in_=t["us", n][:], func=RELU)
            else:
                nc.vector.tensor_scalar(out=uo[:], in0=t["us", n][:], scalar1=0.0, scalar2=None, op0=MAX)
            f0 = n % 2 * 2 * F
            nc.sync.dma_start(out=u_hbm[n // 2][:, f0 : f0 + 2 * F], in_=uo[:].rearrange("p r f -> p (r f)"))

        stages = {
            "P": product, "TA": turn_a, "EA": empty_a, "QA": quantise_a, "MM": multiply_a, "SB": add_bias,
            "XA": add_x, "NM": negative_mean, "SQ": square, "AR": inverse_std, "NR": scaled_mean, "XH": normalise,
            "TH": turn_h, "EH": empty_h, "IL": interleave, "QB": quantise_h, "M2": multiply_h, "UA": add_u, "RL": relu_u,
        }
        for s in range(PAIRS + max(lag for name, i, lag in SLOT)):
            for name, i, lag in SLOT:
                if 0 <= s - lag < PAIRS:
                    stages[name](s - lag, i)
